import numpy as np
import ml_dtypes


def mxq(x, axis, fmt="e4m3"):
    dtype, down = {"e4m3": (ml_dtypes.float8_e4m3fn, 7), "e5m2": (ml_dtypes.float8_e5m2, 14)}[fmt]
    v = np.moveaxis(np.asarray(x, np.float32).astype(ml_dtypes.bfloat16).astype(np.float64), axis, -1)
    blocks = v.reshape(v.shape[:-1] + (-1, 32))
    amax = np.abs(blocks).max(-1, keepdims=True)
    byte = np.maximum(np.where(amax > 0, np.frexp(amax)[1] - 1 + 127, 0) - down, 1)
    scale = np.exp2(byte - 127.0)
    codes = (blocks / scale).astype(np.float32).astype(dtype).astype(np.float64)
    return np.moveaxis((codes * scale).reshape(v.shape), -1, axis)


WIDE = False


def mx_kscale(k):
    if not WIDE:
        return np.ones(k)
    levels = np.array([10, -10, 5, -5, 0])
    a = np.random.permutation(np.resize(levels, k // 512 * 4)).reshape(k // 512, 4)
    idx = np.arange(k)
    return np.exp2(a[idx // 512, idx % 128 // 32])


BF16 = ml_dtypes.bfloat16


def bf(x):
    return np.asarray(x, np.float32).astype(BF16)


def f64(x):
    return np.asarray(x).astype(np.float64)


B, H, W, CIN, COUT = 256, 2, 4, 512, 32
P = H * W


def setup_inputs():
    s = mx_kscale(CIN)
    return {"inputs": bf(np.random.standard_normal((B, H, W, CIN)) * s),
            "kernel": bf(np.random.standard_normal((H, W, CIN, H, W, COUT)) / np.sqrt(CIN) / s[None, None, :, None, None, None]),
            "bias": bf(np.random.standard_normal((H, W, COUT)) * 0.5)}


def reference(inputs, kernel, bias):
    x = f64(inputs).reshape(B, P, CIN).transpose(1, 0, 2)
    k4 = f64(kernel).reshape(P, CIN, P, COUT)
    idx = np.arange(P)
    kd = k4[idx, :, idx, :]
    out = mxq(x, 2, "e4m3") @ mxq(kd, 1, "e4m3")
    return out.transpose(1, 0, 2).reshape(B, H, W, COUT) + f64(bias)

@@ -1,0 +1,138 @@
+from contextlib import ExitStack
+
+import concourse.mybir as mybir
+from concourse.masks import make_identity
+
+BF16 = mybir.dt.bfloat16
+F32 = mybir.dt.float32
+I32 = mybir.dt.int32
+U32 = mybir.dt.uint32
+U8 = mybir.dt.uint8
+FP8X4 = mybir.dt.float8_e4m3fn_x4
+
+P = 128
+PACK = 4
+BATCH = 256
+PLACES = 8
+CIN = 512
+COUT = 32
+BATCH_TILES = BATCH // P
+QUAD = P // COUT
+QUADS = PLACES // QUAD
+PAIR = 2
+HALVES = 2
+
+FLOPS = 2 * BATCH * PLACES * CIN * COUT
+BYTES = 2 * BATCH * PLACES * CIN + 2 * PLACES * CIN * COUT + 2 * PLACES * COUT + 4 * BATCH * PLACES * COUT
+
+
+def tile_locallyconnected2d_s_kernel(tc, inputs, kernel, bias, out):
+    nc = tc.nc
+    x_dram = inputs.rearrange("(t b) i j k -> t b (i j k)", b=P)
+    w_dram = kernel.rearrange("i j k a b c -> (i j) k (a b) c")
+    bias_row = bias.rearrange("i j c -> (i j c)")
+    out_dram = out.rearrange("(t b) i j c -> t b (i j c)", b=P)
+
+    with ExitStack() as ctx:
+        keep = ctx.enter_context(tc.tile_pool(name="keep", bufs=1))
+        x_pool = ctx.enter_context(tc.tile_pool(name="x_pool", bufs=BATCH_TILES * QUADS))
+        grouped_pool = ctx.enter_context(tc.tile_pool(name="grouped_pool", bufs=3))
+        flipped_pool = ctx.enter_context(tc.psum_pool(name="flipped_pool", bufs=6))
+        acc_pool = ctx.enter_context(tc.psum_pool(name="acc_pool", bufs=1))
+
+        x_raw = {}
+        for quad in range(QUADS):
+            for t in range(BATCH_TILES):
+                x_chunk = x_pool.tile([P, QUAD * CIN], BF16)
+                nc.sync.dma_start(
+                    out=x_chunk[:], in_=x_dram[t, :, quad * QUAD * CIN : (quad + 1) * QUAD * CIN]
+                )
+                x_raw[(t, quad)] = x_chunk
+
+        w_raw = keep.tile([P, PLACES, PACK, COUT], BF16)
+        for place in range(PLACES):
+            nc.sync.dma_start(
+                out=w_raw[:, place, :, :],
+                in_=w_dram[place, :, place, :].rearrange("(q j) c -> q j c", j=PACK),
+            )
+
+        bias_all = keep.tile([P, PLACES * COUT], BF16)
+        nc.scalar.dma_start(out=bias_all[:], in_=bias_row.partition_broadcast(P))
+
+        ident = keep.tile([P, P], F32)
+        make_identity(nc, ident[:])
+
+        w_grouped = keep.tile([P, PLACES, P, PACK], BF16, align_bytes=64)
+        nc.vector.memset(w_grouped[:].rearrange("q s n j -> q (s n j)").bitcast(I32), 0)
+
+        x_codes = keep.tile([P, BATCH_TILES * PLACES * P], U32, align_bytes=64)
+        x_scales = keep.tile([P, BATCH_TILES * PLACES * P], U8, align_bytes=64)
+        w_codes = keep.tile([P, PLACES * P], U32, align_bytes=64)
+        w_scales = keep.tile([P, PLACES * P], U8, align_bytes=64)
+
+        for quad in range(QUADS):
+            for t in range(BATCH_TILES):
+                x_words = (
+                    x_raw[(t, quad)][:]
+                    .bitcast(F32)
+                    .rearrange("b (s q h) -> b s h q", q=P, h=HALVES)
+                )
+                for pair in range(QUAD // PAIR):
+                    flipped = flipped_pool.tile([P, PAIR, HALVES, P], F32)
+                    for s in range(PAIR):
+                        for h in range(HALVES):
+                            nc.tensor.transpose(
+                                flipped[:, s, h, :], x_words[:, pair * PAIR + s, h, :], ident[:]
+                            )
+                    x_grouped = grouped_pool.tile([P, PAIR * P * PACK], BF16, align_bytes=64)
+                    grouped_words = x_grouped[:].bitcast(F32).rearrange(
+                        "q (s b h) -> q s b h", s=PAIR, h=HALVES
+                    )
+                    flipped_words = flipped[:].rearrange("q s h b -> q s b h")
+                    if pair % 2 == 0:
+                        nc.scalar.copy(out=grouped_words, in_=flipped_words)
+                    else:
+                        nc.vector.tensor_copy(out=grouped_words, in_=flipped_words)
+                    first = (t * PLACES + quad * QUAD + pair * PAIR) * P
+                    nc.vector.quantize_mx(
+                        out=x_codes[:, first : first + PAIR * P].bitcast(FP8X4),
+                        scales=x_scales[:, first : first + PAIR * P],
+                        in_=x_grouped[:],
+                    )
+
+        acc = [acc_pool.tile([P, PLACES * COUT], F32, name="acc%d" % t) for t in range(BATCH_TILES)]
+        result = [keep.tile([P, PLACES * COUT], F32, name="result%d" % t) for t in range(BATCH_TILES)]
+        for place in range(PLACES):
+            quad = place // QUAD
+            slot = place % QUAD
+            nc.vector.tensor_copy(
+                out=w_grouped[:, place, slot * COUT : (slot + 1) * COUT, :],
+                in_=w_raw[:, place, :, :].rearrange("q j c -> q c j"),
+            )
+            w_cols = slice(place * P, (place + 1) * P)
+            nc.vector.quantize_mx(
+                out=w_codes[:, w_cols].bitcast(FP8X4),
+                scales=w_scales[:, w_cols],
+                in_=w_grouped[:, place, :, :].rearrange("q n j -> q (n j)"),
+            )
+            out_cols = slice(quad * P, (quad + 1) * P)
+            for t in range(BATCH_TILES):
+                x_cols = slice((t * PLACES + place) * P, (t * PLACES + place + 1) * P)
+                nc.tensor.matmul_mx(
+                    out=acc[t][:, out_cols],
+                    lhsT=x_codes[:, x_cols].bitcast(FP8X4),
+                    lhsT_scale=x_scales[:, x_cols],
+                    rhs=w_codes[:, w_cols].bitcast(FP8X4),
+                    rhs_scale=w_scales[:, w_cols],
+                    start=(slot == 0),
+                    stop=(slot == QUAD - 1),
+                )
+            if slot == QUAD - 1:
+                for t in range(BATCH_TILES):
+                    nc.vector.tensor_tensor(
+                        out=result[t][:, out_cols],
+                        in0=acc[t][:, out_cols],
+                        in1=bias_all[:, out_cols],
+                        op=mybir.AluOpType.add,
+                    )
+                    nc.sync.dma_start(out=out_dram[t, :, out_cols], in_=result[t][:, out_cols])

@@ -56,11 +56,23 @@ def tile_locallyconnected2d_s_kernel(tc, inputs, kernel, bias, out):
                 in_=w_dram[place, :, place, :].rearrange("(q j) c -> q j c", j=PACK),
             )
 
-        bias_all = keep.tile([P, PLACES * COUT], BF16)
-        nc.scalar.dma_start(out=bias_all[:], in_=bias_row.partition_broadcast(P))
-
         ident = keep.tile([P, P], F32)
         make_identity(nc, ident[:])
+
+        bias_pairs = keep.tile([P, 2], BF16)
+        nc.scalar.dma_start(out=bias_pairs[:], in_=bias_row.rearrange("(n e) -> n e", e=2))
+        bias_columns = keep.tile([P, 2], F32)
+        nc.vector.tensor_copy(out=bias_columns[:], in_=bias_pairs[:])
+        bias_spread = flipped_pool.tile([P, 2, P], F32, tag="flipped")
+        for e in range(2):
+            nc.tensor.transpose(
+                bias_spread[:, e, :], bias_columns[:, e : e + 1].to_broadcast([P, P]), ident[:]
+            )
+        bias_all = keep.tile([P, PLACES * COUT], F32)
+        nc.vector.tensor_copy(
+            out=bias_all[:].rearrange("p (n e) -> p n e", e=2),
+            in_=bias_spread[:].rearrange("p e n -> p n e"),
+        )
 
         w_grouped = keep.tile([P, PLACES, P, PACK], BF16, align_bytes=64)
         nc.vector.memset(w_grouped[:].rearrange("q s n j -> q (s n j)").bitcast(I32), 0)

@@ -21,6 +21,8 @@ QUAD = P // COUT
 QUADS = PLACES // QUAD
 PAIR = 2
 HALVES = 2
+ROUNDS = BATCH_TILES * PLACES // PAIR
+LEAD = 4
 
 FLOPS = 2 * BATCH * PLACES * CIN * COUT
 BYTES = 2 * BATCH * PLACES * CIN + 2 * PLACES * CIN * COUT + 2 * PLACES * COUT + 4 * BATCH * PLACES * COUT
@@ -35,20 +37,18 @@ def tile_locallyconnected2d_s_kernel(tc, inputs, kernel, bias, out):
 
     with ExitStack() as ctx:
         keep = ctx.enter_context(tc.tile_pool(name="keep", bufs=1))
-        x_pool = ctx.enter_context(tc.tile_pool(name="x_pool", bufs=BATCH_TILES * QUADS))
-        grouped_pool = ctx.enter_context(tc.tile_pool(name="grouped_pool", bufs=3))
+        grouped_pool = ctx.enter_context(tc.tile_pool(name="grouped_pool", bufs=4))
         flipped_pool = ctx.enter_context(tc.psum_pool(name="flipped_pool", bufs=6))
         acc_pool = ctx.enter_context(tc.psum_pool(name="acc_pool", bufs=1))
+        ctx.enter_context(tc.manual_schedule())
 
-        x_raw = {}
+        x_raw = keep.tile([P, QUADS, BATCH_TILES, QUAD * CIN], BF16)
         for quad in range(QUADS):
             for t in range(BATCH_TILES):
-                x_chunk = x_pool.tile([P, QUAD * CIN], BF16)
                 nc.sync.dma_start(
-                    out=x_chunk[:], in_=x_dram[t, :, quad * QUAD * CIN : (quad + 1) * QUAD * CIN]
+                    out=x_raw[:, quad, t, :],
+                    in_=x_dram[t, :, quad * QUAD * CIN : (quad + 1) * QUAD * CIN],
                 )
-                x_raw[(t, quad)] = x_chunk
-
         w_raw = keep.tile([P, PLACES, PACK, COUT], BF16)
         for place in range(PLACES):
             nc.sync.dma_start(
@@ -58,6 +58,9 @@ def tile_locallyconnected2d_s_kernel(tc, inputs, kernel, bias, out):
 
         ident = keep.tile([P, P], F32)
         make_identity(nc, ident[:])
+
+        w_grouped = keep.tile([P, PLACES, P, PACK], BF16, align_bytes=64)
+        nc.vector.memset(w_grouped[:].rearrange("q s n j -> q (s n j)").bitcast(I32), 0)
 
         bias_pairs = keep.tile([P, 2], BF16)
         nc.scalar.dma_start(out=bias_pairs[:], in_=bias_row.rearrange("(n e) -> n e", e=2))
@@ -74,77 +77,73 @@ def tile_locallyconnected2d_s_kernel(tc, inputs, kernel, bias, out):
             in_=bias_spread[:].rearrange("p e n -> p n e"),
         )
 
-        w_grouped = keep.tile([P, PLACES, P, PACK], BF16, align_bytes=64)
-        nc.vector.memset(w_grouped[:].rearrange("q s n j -> q (s n j)").bitcast(I32), 0)
-
         x_codes = keep.tile([P, BATCH_TILES * PLACES * P], U32, align_bytes=64)
         x_scales = keep.tile([P, BATCH_TILES * PLACES * P], U8, align_bytes=64)
         w_codes = keep.tile([P, PLACES * P], U32, align_bytes=64)
         w_scales = keep.tile([P, PLACES * P], U8, align_bytes=64)
 
-        for quad in range(QUADS):
-            for t in range(BATCH_TILES):
-                x_words = (
-                    x_raw[(t, quad)][:]
-                    .bitcast(F32)
-                    .rearrange("b (s q h) -> b s h q", q=P, h=HALVES)
-                )
-                for pair in range(QUAD // PAIR):
-                    flipped = flipped_pool.tile([P, PAIR, HALVES, P], F32)
-                    for s in range(PAIR):
-                        for h in range(HALVES):
-                            nc.tensor.transpose(
-                                flipped[:, s, h, :], x_words[:, pair * PAIR + s, h, :], ident[:]
-                            )
-                    x_grouped = grouped_pool.tile([P, PAIR * P * PACK], BF16, align_bytes=64)
-                    grouped_words = x_grouped[:].bitcast(F32).rearrange(
-                        "q (s b h) -> q s b h", s=PAIR, h=HALVES
-                    )
-                    flipped_words = flipped[:].rearrange("q s h b -> q s b h")
-                    if pair % 2 == 0:
-                        nc.scalar.copy(out=grouped_words, in_=flipped_words)
-                    else:
-                        nc.vector.tensor_copy(out=grouped_words, in_=flipped_words)
-                    first = (t * PLACES + quad * QUAD + pair * PAIR) * P
-                    nc.vector.quantize_mx(
-                        out=x_codes[:, first : first + PAIR * P].bitcast(FP8X4),
-                        scales=x_scales[:, first : first + PAIR * P],
-                        in_=x_grouped[:],
-                    )
+        def quantise_activations(rnd):
+            quad = rnd // (BATCH_TILES * QUAD // PAIR)
+            t = rnd // (QUAD // PAIR) % BATCH_TILES
+            pair = rnd % (QUAD // PAIR)
+            x_words = x_raw[:, quad, t, :].bitcast(F32).rearrange("b (s q h) -> b s h q", q=P, h=HALVES)
+            flipped = flipped_pool.tile([P, PAIR, HALVES, P], F32)
+            for s in range(PAIR):
+                for h in range(HALVES):
+                    nc.tensor.transpose(flipped[:, s, h, :], x_words[:, pair * PAIR + s, h, :], ident[:])
+            x_grouped = grouped_pool.tile([P, PAIR * P * PACK], BF16, align_bytes=64)
+            nc.scalar.copy(
+                out=x_grouped[:].bitcast(F32).rearrange("q (s b h) -> q s b h", s=PAIR, h=HALVES),
+                in_=flipped[:].rearrange("q s h b -> q s b h"),
+            )
+            first = (t * PLACES + quad * QUAD + pair * PAIR) * P
+            nc.vector.quantize_mx(
+                out=x_codes[:, first : first + PAIR * P].bitcast(FP8X4),
+                scales=x_scales[:, first : first + PAIR * P],
+                in_=x_grouped[:],
+            )
 
-        acc = [acc_pool.tile([P, PLACES * COUT], F32, name="acc%d" % t) for t in range(BATCH_TILES)]
-        result = [keep.tile([P, PLACES * COUT], F32, name="result%d" % t) for t in range(BATCH_TILES)]
-        for place in range(PLACES):
-            quad = place // QUAD
+        def quantise_weights(place):
             slot = place % QUAD
             nc.vector.tensor_copy(
                 out=w_grouped[:, place, slot * COUT : (slot + 1) * COUT, :],
                 in_=w_raw[:, place, :, :].rearrange("q j c -> q c j"),
             )
-            w_cols = slice(place * P, (place + 1) * P)
             nc.vector.quantize_mx(
-                out=w_codes[:, w_cols].bitcast(FP8X4),
-                scales=w_scales[:, w_cols],
+                out=w_codes[:, place * P : (place + 1) * P].bitcast(FP8X4),
+                scales=w_scales[:, place * P : (place + 1) * P],
                 in_=w_grouped[:, place, :, :].rearrange("q n j -> q (n j)"),
             )
-            out_cols = slice(quad * P, (quad + 1) * P)
+
+        for step in range(LEAD + PLACES):
+            if step < ROUNDS:
+                quantise_activations(step)
+            if step >= LEAD:
+                quantise_weights(step - LEAD)
+
+        acc = [acc_pool.tile([P, PLACES * COUT], F32, name="acc%d" % t) for t in range(BATCH_TILES)]
+        for place in range(PLACES):
             for t in range(BATCH_TILES):
                 x_cols = slice((t * PLACES + place) * P, (t * PLACES + place + 1) * P)
+                w_cols = slice(place * P, (place + 1) * P)
                 nc.tensor.matmul_mx(
-                    out=acc[t][:, out_cols],
+                    out=acc[t][:, place // QUAD * P : (place // QUAD + 1) * P],
                     lhsT=x_codes[:, x_cols].bitcast(FP8X4),
                     lhsT_scale=x_scales[:, x_cols],
                     rhs=w_codes[:, w_cols].bitcast(FP8X4),
                     rhs_scale=w_scales[:, w_cols],
-                    start=(slot == 0),
-                    stop=(slot == QUAD - 1),
+                    start=(place % QUAD == 0),
+                    stop=(place % QUAD == QUAD - 1),
                 )
-            if slot == QUAD - 1:
-                for t in range(BATCH_TILES):
-                    nc.vector.tensor_tensor(
-                        out=result[t][:, out_cols],
-                        in0=acc[t][:, out_cols],
-                        in1=bias_all[:, out_cols],
-                        op=mybir.AluOpType.add,
-                    )
-                    nc.sync.dma_start(out=out_dram[t, :, out_cols], in_=result[t][:, out_cols])
+
+        result = [keep.tile([P, PLACES * COUT], F32, name="result%d" % t) for t in range(BATCH_TILES)]
+        for quad in range(QUADS):
+            out_cols = slice(quad * P, (quad + 1) * P)
+            for t in range(BATCH_TILES):
+                nc.vector.tensor_tensor(
+                    out=result[t][:, out_cols],
+                    in0=acc[t][:, out_cols],
+                    in1=bias_all[:, out_cols],
+                    op=mybir.AluOpType.add,
+                )
+                nc.sync.dma_start(out=out_dram[t, :, out_cols], in_=result[t][:, out_cols])

@@ -66,16 +66,18 @@ def tile_locallyconnected2d_s_kernel(tc, inputs, kernel, bias, out):
         nc.scalar.dma_start(out=bias_pairs[:], in_=bias_row.rearrange("(n e) -> n e", e=2))
         bias_columns = keep.tile([P, 2], F32)
         nc.vector.tensor_copy(out=bias_columns[:], in_=bias_pairs[:])
-        bias_spread = flipped_pool.tile([P, 2, P], F32, tag="flipped")
-        for e in range(2):
-            nc.tensor.transpose(
-                bias_spread[:, e, :], bias_columns[:, e : e + 1].to_broadcast([P, P]), ident[:]
-            )
         bias_all = keep.tile([P, PLACES * COUT], F32)
-        nc.vector.tensor_copy(
-            out=bias_all[:].rearrange("p (n e) -> p n e", e=2),
-            in_=bias_spread[:].rearrange("p e n -> p n e"),
-        )
+
+        def spread_bias():
+            bias_spread = flipped_pool.tile([P, 2, P], F32, tag="flipped")
+            for e in range(2):
+                nc.tensor.transpose(
+                    bias_spread[:, e, :], bias_columns[:, e : e + 1].to_broadcast([P, P]), ident[:]
+                )
+            nc.vector.tensor_copy(
+                out=bias_all[:].rearrange("p (n e) -> p n e", e=2),
+                in_=bias_spread[:].rearrange("p e n -> p n e"),
+            )
 
         x_codes = keep.tile([P, BATCH_TILES * PLACES * P], U32, align_bytes=64)
         x_scales = keep.tile([P, BATCH_TILES * PLACES * P], U8, align_bytes=64)
@@ -103,23 +105,32 @@ def tile_locallyconnected2d_s_kernel(tc, inputs, kernel, bias, out):
                 in_=x_grouped[:],
             )
 
-        def quantise_weights(place):
+        def regroup_weights(place):
             slot = place % QUAD
-            nc.vector.tensor_copy(
-                out=w_grouped[:, place, slot * COUT : (slot + 1) * COUT, :],
-                in_=w_raw[:, place, :, :].rearrange("q j c -> q c j"),
-            )
+            own_columns = w_grouped[:, place, slot * COUT : (slot + 1) * COUT, :]
+            by_column = w_raw[:, place, :, :].rearrange("q j c -> q c j")
+            if place < QUAD:
+                nc.vector.tensor_copy(out=own_columns, in_=by_column)
+            else:
+                nc.scalar.copy(out=own_columns, in_=by_column)
+
+        def quantise_weights(place):
             nc.vector.quantize_mx(
                 out=w_codes[:, place * P : (place + 1) * P].bitcast(FP8X4),
                 scales=w_scales[:, place * P : (place + 1) * P],
                 in_=w_grouped[:, place, :, :].rearrange("q n j -> q (n j)"),
             )
 
-        for step in range(LEAD + PLACES):
-            if step < ROUNDS:
-                quantise_activations(step)
-            if step >= LEAD:
-                quantise_weights(step - LEAD)
+        for rnd in range(LEAD):
+            quantise_activations(rnd)
+        spread_bias()
+        for place in range(PLACES):
+            if place + LEAD < ROUNDS:
+                quantise_activations(place + LEAD)
+            regroup_weights(place)
+            if place > 0:
+                quantise_weights(place - 1)
+        quantise_weights(PLACES - 1)
 
         acc = [acc_pool.tile([P, PLACES * COUT], F32, name="acc%d" % t) for t in range(BATCH_TILES)]
         for place in range(PLACES):

@@ -17,7 +17,7 @@ PLACES = 8
 CIN = 512
 COUT = 32
 BATCH_TILES = BATCH // P
-QUAD = P // COUT
+QUAD = 4
 QUADS = PLACES // QUAD
 PAIR = 2
 HALVES = 2
@@ -38,7 +38,7 @@ def tile_locallyconnected2d_s_kernel(tc, inputs, kernel, bias, out):
     with ExitStack() as ctx:
         keep = ctx.enter_context(tc.tile_pool(name="keep", bufs=1))
         grouped_pool = ctx.enter_context(tc.tile_pool(name="grouped_pool", bufs=4))
-        flipped_pool = ctx.enter_context(tc.psum_pool(name="flipped_pool", bufs=6))
+        flipped_pool = ctx.enter_context(tc.psum_pool(name="flipped_pool", bufs=4))
         acc_pool = ctx.enter_context(tc.psum_pool(name="acc_pool", bufs=1))
         ctx.enter_context(tc.manual_schedule())
 
@@ -59,8 +59,11 @@ def tile_locallyconnected2d_s_kernel(tc, inputs, kernel, bias, out):
         ident = keep.tile([P, P], F32)
         make_identity(nc, ident[:])
 
-        w_grouped = keep.tile([P, PLACES, P, PACK], BF16, align_bytes=64)
-        nc.vector.memset(w_grouped[:].rearrange("q s n j -> q (s n j)").bitcast(I32), 0)
+        w_codes = keep.tile([P, PLACES, P], U32, align_bytes=64)
+        w_scales = keep.tile([P, PLACES, P], U8, align_bytes=64)
+        nc.vector.memset(w_codes[:].rearrange("q s n -> q (s n)").bitcast(I32), 0)
+        nc.vector.memset(w_scales[:].rearrange("q s n -> q (s n)").bitcast(I32), 0)
+        w_grouped = keep.tile([P, PLACES, COUT, PACK], BF16, align_bytes=64)
 
         bias_pairs = keep.tile([P, 2], BF16)
         nc.scalar.dma_start(out=bias_pairs[:], in_=bias_row.rearrange("(n e) -> n e", e=2))
@@ -81,8 +84,6 @@ def tile_locallyconnected2d_s_kernel(tc, inputs, kernel, bias, out):
 
         x_codes = keep.tile([P, BATCH_TILES * PLACES * P], U32, align_bytes=64)
         x_scales = keep.tile([P, BATCH_TILES * PLACES * P], U8, align_bytes=64)
-        w_codes = keep.tile([P, PLACES * P], U32, align_bytes=64)
-        w_scales = keep.tile([P, PLACES * P], U8, align_bytes=64)
 
         def quantise_activations(rnd):
             quad = rnd // (BATCH_TILES * QUAD // PAIR)
@@ -106,8 +107,7 @@ def tile_locallyconnected2d_s_kernel(tc, inputs, kernel, bias, out):
             )
 
         def regroup_weights(place):
-            slot = place % QUAD
-            own_columns = w_grouped[:, place, slot * COUT : (slot + 1) * COUT, :]
+            own_columns = w_grouped[:, place, :, :]
             by_column = w_raw[:, place, :, :].rearrange("q j c -> q c j")
             if place < QUAD:
                 nc.vector.tensor_copy(out=own_columns, in_=by_column)
@@ -116,9 +116,9 @@ def tile_locallyconnected2d_s_kernel(tc, inputs, kernel, bias, out):
 
         def quantise_weights(place):
             nc.vector.quantize_mx(
-                out=w_codes[:, place * P : (place + 1) * P].bitcast(FP8X4),
-                scales=w_scales[:, place * P : (place + 1) * P],
-                in_=w_grouped[:, place, :, :].rearrange("q n j -> q (n j)"),
+                out=w_codes[:, place, 0:COUT].bitcast(FP8X4),
+                scales=w_scales[:, place, 0:COUT],
+                in_=w_grouped[:, place, :, :].rearrange("q c j -> q (c j)"),
             )
 
         for rnd in range(LEAD):
@@ -132,29 +132,31 @@ def tile_locallyconnected2d_s_kernel(tc, inputs, kernel, bias, out):
                 quantise_weights(place - 1)
         quantise_weights(PLACES - 1)
 
-        acc = [acc_pool.tile([P, PLACES * COUT], F32, name="acc%d" % t) for t in range(BATCH_TILES)]
+        acc = {}
+        for quad in range(QUADS):
+            for t in range(BATCH_TILES):
+                acc[(t, quad)] = acc_pool.tile([P, QUAD, P], F32, name="acc%d%d" % (t, quad))
         for place in range(PLACES):
             for t in range(BATCH_TILES):
                 x_cols = slice((t * PLACES + place) * P, (t * PLACES + place + 1) * P)
-                w_cols = slice(place * P, (place + 1) * P)
                 nc.tensor.matmul_mx(
-                    out=acc[t][:, place // QUAD * P : (place // QUAD + 1) * P],
+                    out=acc[(t, place // QUAD)][:, place % QUAD, :],
                     lhsT=x_codes[:, x_cols].bitcast(FP8X4),
                     lhsT_scale=x_scales[:, x_cols],
-                    rhs=w_codes[:, w_cols].bitcast(FP8X4),
-                    rhs_scale=w_scales[:, w_cols],
-                    start=(place % QUAD == 0),
-                    stop=(place % QUAD == QUAD - 1),
+                    rhs=w_codes[:, place, :].bitcast(FP8X4),
+                    rhs_scale=w_scales[:, place, :],
+                    start=True,
+                    stop=True,
                 )
 
         result = [keep.tile([P, PLACES * COUT], F32, name="result%d" % t) for t in range(BATCH_TILES)]
         for quad in range(QUADS):
-            out_cols = slice(quad * P, (quad + 1) * P)
+            out_cols = slice(quad * QUAD * COUT, (quad + 1) * QUAD * COUT)
             for t in range(BATCH_TILES):
                 nc.vector.tensor_tensor(
-                    out=result[t][:, out_cols],
-                    in0=acc[t][:, out_cols],
-                    in1=bias_all[:, out_cols],
+                    out=result[t][:, out_cols].rearrange("b (s c) -> b s c", c=COUT),
+                    in0=acc[(t, quad)][:, :, 0:COUT],
+                    in1=bias_all[:, out_cols].rearrange("b (s c) -> b s c", c=COUT),
                     op=mybir.AluOpType.add,
                 )
                 nc.sync.dma_start(out=out_dram[t, :, out_cols], in_=result[t][:, out_cols])

@@ -23,6 +23,7 @@ PAIR = 2
 HALVES = 2
 ROUNDS = BATCH_TILES * PLACES // PAIR
 LEAD = 4
+VECTOR_ROUNDS = (2, 5)
 
 FLOPS = 2 * BATCH * PLACES * CIN * COUT
 BYTES = 2 * BATCH * PLACES * CIN + 2 * PLACES * CIN * COUT + 2 * PLACES * COUT + 4 * BATCH * PLACES * COUT
@@ -85,7 +86,10 @@ def tile_locallyconnected2d_s_kernel(tc, inputs, kernel, bias, out):
         x_codes = keep.tile([P, BATCH_TILES * PLACES * P], U32, align_bytes=64)
         x_scales = keep.tile([P, BATCH_TILES * PLACES * P], U8, align_bytes=64)
 
-        def quantise_activations(rnd):
+        flipped_banks = {}
+        grouped_tiles = {}
+
+        def flip(rnd):
             quad = rnd // (BATCH_TILES * QUAD // PAIR)
             t = rnd // (QUAD // PAIR) % BATCH_TILES
             pair = rnd % (QUAD // PAIR)
@@ -94,16 +98,26 @@ def tile_locallyconnected2d_s_kernel(tc, inputs, kernel, bias, out):
             for s in range(PAIR):
                 for h in range(HALVES):
                     nc.tensor.transpose(flipped[:, s, h, :], x_words[:, pair * PAIR + s, h, :], ident[:])
+            flipped_banks[rnd] = flipped
+
+        def empty(rnd):
             x_grouped = grouped_pool.tile([P, PAIR * P * PACK], BF16, align_bytes=64)
-            nc.scalar.copy(
+            copy = nc.vector.tensor_copy if rnd in VECTOR_ROUNDS else nc.scalar.copy
+            copy(
                 out=x_grouped[:].bitcast(F32).rearrange("q (s b h) -> q s b h", s=PAIR, h=HALVES),
-                in_=flipped[:].rearrange("q s h b -> q s b h"),
+                in_=flipped_banks[rnd][:].rearrange("q s h b -> q s b h"),
             )
+            grouped_tiles[rnd] = x_grouped
+
+        def quantise(rnd):
+            quad = rnd // (BATCH_TILES * QUAD // PAIR)
+            t = rnd // (QUAD // PAIR) % BATCH_TILES
+            pair = rnd % (QUAD // PAIR)
             first = (t * PLACES + quad * QUAD + pair * PAIR) * P
             nc.vector.quantize_mx(
                 out=x_codes[:, first : first + PAIR * P].bitcast(FP8X4),
                 scales=x_scales[:, first : first + PAIR * P],
-                in_=x_grouped[:],
+                in_=grouped_tiles[rnd][:],
             )
 
         def regroup_weights(place):
@@ -122,11 +136,20 @@ def tile_locallyconnected2d_s_kernel(tc, inputs, kernel, bias, out):
             )
 
         for rnd in range(LEAD):
-            quantise_activations(rnd)
+            flip(rnd)
+            empty(rnd)
+            if rnd > 0:
+                quantise(rnd - 1)
         spread_bias()
+        flip(LEAD)
+        empty(LEAD)
+        quantise(LEAD - 1)
         for place in range(PLACES):
+            if place + LEAD + 1 < ROUNDS:
+                flip(place + LEAD + 1)
+                empty(place + LEAD + 1)
             if place + LEAD < ROUNDS:
-                quantise_activations(place + LEAD)
+                quantise(place + LEAD)
             regroup_weights(place)
             if place > 0:
                 quantise_weights(place - 1)

@@ -144,15 +144,28 @@ def tile_locallyconnected2d_s_kernel(tc, inputs, kernel, bias, out):
         flip(LEAD)
         empty(LEAD)
         quantise(LEAD - 1)
-        for place in range(PLACES):
-            if place + LEAD + 1 < ROUNDS:
-                flip(place + LEAD + 1)
-                empty(place + LEAD + 1)
-            if place + LEAD < ROUNDS:
-                quantise(place + LEAD)
+        flip(5)
+        empty(5)
+        quantise(4)
+        regroup_weights(0)
+        flip(6)
+        empty(6)
+        quantise(5)
+        regroup_weights(1)
+        quantise_weights(0)
+        regroup_weights(2)
+        quantise_weights(1)
+        flip(7)
+        empty(7)
+        quantise(6)
+        regroup_weights(3)
+        quantise_weights(2)
+        regroup_weights(4)
+        quantise_weights(3)
+        quantise(7)
+        for place in range(5, PLACES):
             regroup_weights(place)
-            if place > 0:
-                quantise_weights(place - 1)
+            quantise_weights(place - 1)
         quantise_weights(PLACES - 1)
 
         acc = {}

@@ -23,7 +23,7 @@ PAIR = 2
 HALVES = 2
 ROUNDS = BATCH_TILES * PLACES // PAIR
 LEAD = 4
-VECTOR_ROUNDS = (2, 5)
+VECTOR_ROUNDS = (1, 3)
 
 FLOPS = 2 * BATCH * PLACES * CIN * COUT
 BYTES = 2 * BATCH * PLACES * CIN + 2 * PLACES * CIN * COUT + 2 * PLACES * COUT + 4 * BATCH * PLACES * COUT

@@ -23,6 +23,8 @@ PAIR = 2
 HALVES = 2
 ROUNDS = BATCH_TILES * PLACES // PAIR
 LEAD = 4
+BANK = 512
+GROUPS = ((0, 4), (4, 7), (7, 8))
 VECTOR_ROUNDS = (1, 3)
 
 FLOPS = 2 * BATCH * PLACES * CIN * COUT
@@ -34,7 +36,7 @@ def tile_locallyconnected2d_s_kernel(tc, inputs, kernel, bias, out):
     x_dram = inputs.rearrange("(t b) i j k -> t b (i j k)", b=P)
     w_dram = kernel.rearrange("i j k a b c -> (i j) k (a b) c")
     bias_row = bias.rearrange("i j c -> (i j c)")
-    out_dram = out.rearrange("(t b) i j c -> t b (i j c)", b=P)
+    out_rows = out.rearrange("(t b) i j c -> b t (i j c)", b=P)
 
     with ExitStack() as ctx:
         keep = ctx.enter_context(tc.tile_pool(name="keep", bufs=1))
@@ -144,6 +146,41 @@ def tile_locallyconnected2d_s_kernel(tc, inputs, kernel, bias, out):
         flip(LEAD)
         empty(LEAD)
         quantise(LEAD - 1)
+        acc = {}
+        result = {}
+        for first, end in GROUPS:
+            acc[first] = acc_pool.tile([P, BANK], F32, name="acc%d" % first)
+            result[first] = keep.tile([P, BATCH_TILES, (end - first) * COUT], F32, name="result%d" % first)
+
+        def passes(place):
+            first, end = [g for g in GROUPS if g[0] <= place < g[1]][0]
+            span = (end - first - 1) * COUT + P
+            for t in range(BATCH_TILES):
+                x_cols = slice((t * PLACES + place) * P, (t * PLACES + place + 1) * P)
+                start_col = t * span + (place - first) * COUT
+                nc.tensor.matmul_mx(
+                    out=acc[first][:, start_col : start_col + P],
+                    lhsT=x_codes[:, x_cols].bitcast(FP8X4),
+                    lhsT_scale=x_scales[:, x_cols],
+                    rhs=w_codes[:, place, :].bitcast(FP8X4),
+                    rhs_scale=w_scales[:, place, :],
+                    start=True,
+                    stop=True,
+                )
+
+        def finish(first, end):
+            span = (end - first - 1) * COUT + P
+            width = (end - first) * COUT
+            out_cols = slice(first * COUT, end * COUT)
+            nc.vector.tensor_tensor(
+                out=result[first][:],
+                in0=acc[first][:, 0 : BATCH_TILES * span].rearrange("b (t w) -> b t w", t=BATCH_TILES)[:, :, 0:width],
+                in1=bias_all[:, out_cols].unsqueeze(1).to_broadcast([P, BATCH_TILES, width]),
+                op=mybir.AluOpType.add,
+            )
+            nc.sync.dma_start(out=out_rows[:, :, out_cols], in_=result[first][:])
+
+
         flip(5)
         empty(5)
         quantise(4)
@@ -163,36 +200,21 @@ def tile_locallyconnected2d_s_kernel(tc, inputs, kernel, bias, out):
         regroup_weights(4)
         quantise_weights(3)
         quantise(7)
-        for place in range(5, PLACES):
-            regroup_weights(place)
-            quantise_weights(place - 1)
-        quantise_weights(PLACES - 1)
-
-        acc = {}
-        for quad in range(QUADS):
-            for t in range(BATCH_TILES):
-                acc[(t, quad)] = acc_pool.tile([P, QUAD, P], F32, name="acc%d%d" % (t, quad))
-        for place in range(PLACES):
-            for t in range(BATCH_TILES):
-                x_cols = slice((t * PLACES + place) * P, (t * PLACES + place + 1) * P)
-                nc.tensor.matmul_mx(
-                    out=acc[(t, place // QUAD)][:, place % QUAD, :],
-                    lhsT=x_codes[:, x_cols].bitcast(FP8X4),
-                    lhsT_scale=x_scales[:, x_cols],
-                    rhs=w_codes[:, place, :].bitcast(FP8X4),
-                    rhs_scale=w_scales[:, place, :],
-                    start=True,
-                    stop=True,
-                )
-
-        result = [keep.tile([P, PLACES * COUT], F32, name="result%d" % t) for t in range(BATCH_TILES)]
-        for quad in range(QUADS):
-            out_cols = slice(quad * QUAD * COUT, (quad + 1) * QUAD * COUT)
-            for t in range(BATCH_TILES):
-                nc.vector.tensor_tensor(
-                    out=result[t][:, out_cols].rearrange("b (s c) -> b s c", c=COUT),
-                    in0=acc[(t, quad)][:, :, 0:COUT],
-                    in1=bias_all[:, out_cols].rearrange("b (s c) -> b s c", c=COUT),
-                    op=mybir.AluOpType.add,
-                )
-                nc.sync.dma_start(out=out_dram[t, :, out_cols], in_=result[t][:, out_cols])
+        passes(0)
+        passes(1)
+        passes(2)
+        passes(3)
+        regroup_weights(5)
+        quantise_weights(4)
+        passes(4)
+        regroup_weights(6)
+        quantise_weights(5)
+        passes(5)
+        regroup_weights(7)
+        quantise_weights(6)
+        passes(6)
+        quantise_weights(7)
+        passes(7)
+        finish(0, 4)
+        finish(4, 7)
+        finish(7, 8)

@@ -125,7 +125,7 @@ def tile_locallyconnected2d_s_kernel(tc, inputs, kernel, bias, out):
         def regroup_weights(place):
             own_columns = w_grouped[:, place, :, :]
             by_column = w_raw[:, place, :, :].rearrange("q j c -> q c j")
-            if place < QUAD:
+            if place <= QUAD:
                 nc.vector.tensor_copy(out=own_columns, in_=by_column)
             else:
                 nc.scalar.copy(out=own_columns, in_=by_column)
@@ -184,35 +184,35 @@ def tile_locallyconnected2d_s_kernel(tc, inputs, kernel, bias, out):
         flip(5)
         empty(5)
         quantise(4)
-        regroup_weights(0)
         flip(6)
         empty(6)
-        quantise(5)
-        regroup_weights(1)
-        quantise_weights(0)
-        regroup_weights(2)
-        quantise_weights(1)
         flip(7)
         empty(7)
-        quantise(6)
-        regroup_weights(3)
+        regroup_weights(0)
+        regroup_weights(1)
+        quantise_weights(0)
+        passes(0)
+        quantise_weights(1)
+        passes(1)
+        regroup_weights(2)
+        quantise(5)
         quantise_weights(2)
+        passes(2)
+        regroup_weights(3)
         regroup_weights(4)
         quantise_weights(3)
-        quantise(7)
-        passes(0)
-        passes(1)
-        passes(2)
         passes(3)
-        regroup_weights(5)
         quantise_weights(4)
+        quantise(6)
         passes(4)
-        regroup_weights(6)
+        regroup_weights(5)
         quantise_weights(5)
         passes(5)
-        regroup_weights(7)
+        quantise(7)
+        regroup_weights(6)
         quantise_weights(6)
         passes(6)
+        regroup_weights(7)
         quantise_weights(7)
         passes(7)
         finish(0, 4)

@@ -24,6 +24,7 @@ HALVES = 2
 ROUNDS = BATCH_TILES * PLACES // PAIR
 LEAD = 4
 BANK = 512
+MOVING = 64
 GROUPS = ((0, 4), (4, 7), (7, 8))
 VECTOR_ROUNDS = (1, 3)
 
@@ -62,8 +63,8 @@ def tile_locallyconnected2d_s_kernel(tc, inputs, kernel, bias, out):
         ident = keep.tile([P, P], F32)
         make_identity(nc, ident[:])
 
-        w_codes = keep.tile([P, PLACES, P], U32, align_bytes=64)
-        w_scales = keep.tile([P, PLACES, P], U8, align_bytes=64)
+        w_codes = keep.tile([P, PLACES, MOVING], U32, align_bytes=64)
+        w_scales = keep.tile([P, PLACES, MOVING], U8, align_bytes=64)
         nc.vector.memset(w_codes[:].rearrange("q s n -> q (s n)").bitcast(I32), 0)
         nc.vector.memset(w_scales[:].rearrange("q s n -> q (s n)").bitcast(I32), 0)
         w_grouped = keep.tile([P, PLACES, COUT, PACK], BF16, align_bytes=64)
@@ -154,12 +155,12 @@ def tile_locallyconnected2d_s_kernel(tc, inputs, kernel, bias, out):
 
         def passes(place):
             first, end = [g for g in GROUPS if g[0] <= place < g[1]][0]
-            span = (end - first - 1) * COUT + P
+            span = (end - first - 1) * COUT + MOVING
             for t in range(BATCH_TILES):
                 x_cols = slice((t * PLACES + place) * P, (t * PLACES + place + 1) * P)
                 start_col = t * span + (place - first) * COUT
                 nc.tensor.matmul_mx(
-                    out=acc[first][:, start_col : start_col + P],
+                    out=acc[first][:, start_col : start_col + MOVING],
                     lhsT=x_codes[:, x_cols].bitcast(FP8X4),
                     lhsT_scale=x_scales[:, x_cols],
                     rhs=w_codes[:, place, :].bitcast(FP8X4),
@@ -169,7 +170,7 @@ def tile_locallyconnected2d_s_kernel(tc, inputs, kernel, bias, out):
                 )
 
         def finish(first, end):
-            span = (end - first - 1) * COUT + P
+            span = (end - first - 1) * COUT + MOVING
             width = (end - first) * COUT
             out_cols = slice(first * COUT, end * COUT)
             nc.vector.tensor_tensor(

from contextlib import ExitStack

import concourse.mybir as mybir
from concourse.masks import make_identity

BF16 = mybir.dt.bfloat16
F32 = mybir.dt.float32
I32 = mybir.dt.int32
U32 = mybir.dt.uint32
U8 = mybir.dt.uint8
FP8X4 = mybir.dt.float8_e4m3fn_x4

P = 128
PACK = 4
BATCH = 256
PLACES = 8
CIN = 512
COUT = 32
BATCH_TILES = BATCH // P
QUAD = 4
QUADS = PLACES // QUAD
PAIR = 2
HALVES = 2
ROUNDS = BATCH_TILES * PLACES // PAIR
LEAD = 4
BANK = 512
MOVING = 64
GROUPS = ((0, 4), (4, 7), (7, 8))
VECTOR_ROUNDS = (1, 3)

FLOPS = 2 * BATCH * PLACES * CIN * COUT
BYTES = 2 * BATCH * PLACES * CIN + 2 * PLACES * CIN * COUT + 2 * PLACES * COUT + 4 * BATCH * PLACES * COUT


def tile_locallyconnected2d_s_kernel(tc, inputs, kernel, bias, out):
    nc = tc.nc
    x_dram = inputs.rearrange("(t b) i j k -> t b (i j k)", b=P)
    w_dram = kernel.rearrange("i j k a b c -> (i j) k (a b) c")
    bias_row = bias.rearrange("i j c -> (i j c)")
    out_rows = out.rearrange("(t b) i j c -> b t (i j c)", b=P)

    with ExitStack() as ctx:
        keep = ctx.enter_context(tc.tile_pool(name="keep", bufs=1))
        grouped_pool = ctx.enter_context(tc.tile_pool(name="grouped_pool", bufs=4))
        flipped_pool = ctx.enter_context(tc.psum_pool(name="flipped_pool", bufs=4))
        acc_pool = ctx.enter_context(tc.psum_pool(name="acc_pool", bufs=1))
        ctx.enter_context(tc.manual_schedule())

        x_raw = keep.tile([P, QUADS, BATCH_TILES, QUAD * CIN], BF16)
        for quad in range(QUADS):
            for t in range(BATCH_TILES):
                nc.sync.dma_start(
                    out=x_raw[:, quad, t, :],
                    in_=x_dram[t, :, quad * QUAD * CIN : (quad + 1) * QUAD * CIN],
                )
        w_raw = keep.tile([P, PLACES, PACK, COUT], BF16)
        for place in range(PLACES):
            nc.sync.dma_start(
                out=w_raw[:, place, :, :],
                in_=w_dram[place, :, place, :].rearrange("(q j) c -> q j c", j=PACK),
            )

        ident = keep.tile([P, P], F32)
        make_identity(nc, ident[:])

        w_codes = keep.tile([P, PLACES, MOVING], U32, align_bytes=64)
        w_scales = keep.tile([P, PLACES, MOVING], U8, align_bytes=64)
        nc.vector.memset(w_codes[:].rearrange("q s n -> q (s n)").bitcast(I32), 0)
        nc.vector.memset(w_scales[:].rearrange("q s n -> q (s n)").bitcast(I32), 0)
        w_grouped = keep.tile([P, PLACES, COUT, PACK], BF16, align_bytes=64)

        bias_pairs = keep.tile([P, 2], BF16)
        nc.scalar.dma_start(out=bias_pairs[:], in_=bias_row.rearrange("(n e) -> n e", e=2))
        bias_columns = keep.tile([P, 2], F32)
        nc.vector.tensor_copy(out=bias_columns[:], in_=bias_pairs[:])
        bias_all = keep.tile([P, PLACES * COUT], F32)

        def spread_bias():
            bias_spread = flipped_pool.tile([P, 2, P], F32, tag="flipped")
            for e in range(2):
                nc.tensor.transpose(
                    bias_spread[:, e, :], bias_columns[:, e : e + 1].to_broadcast([P, P]), ident[:]
                )
            nc.vector.tensor_copy(
                out=bias_all[:].rearrange("p (n e) -> p n e", e=2),
                in_=bias_spread[:].rearrange("p e n -> p n e"),
            )

        x_codes = keep.tile([P, BATCH_TILES * PLACES * P], U32, align_bytes=64)
        x_scales = keep.tile([P, BATCH_TILES * PLACES * P], U8, align_bytes=64)

        flipped_banks = {}
        grouped_tiles = {}

        def flip(rnd):
            quad = rnd // (BATCH_TILES * QUAD // PAIR)
            t = rnd // (QUAD // PAIR) % BATCH_TILES
            pair = rnd % (QUAD // PAIR)
            x_words = x_raw[:, quad, t, :].bitcast(F32).rearrange("b (s q h) -> b s h q", q=P, h=HALVES)
            flipped = flipped_pool.tile([P, PAIR, HALVES, P], F32)
            for s in range(PAIR):
                for h in range(HALVES):
                    nc.tensor.transpose(flipped[:, s, h, :], x_words[:, pair * PAIR + s, h, :], ident[:])
            flipped_banks[rnd] = flipped

        def empty(rnd):
            x_grouped = grouped_pool.tile([P, PAIR * P * PACK], BF16, align_bytes=64)
            copy = nc.vector.tensor_copy if rnd in VECTOR_ROUNDS else nc.scalar.copy
            copy(
                out=x_grouped[:].bitcast(F32).rearrange("q (s b h) -> q s b h", s=PAIR, h=HALVES),
                in_=flipped_banks[rnd][:].rearrange("q s h b -> q s b h"),
            )
            grouped_tiles[rnd] = x_grouped

        def quantise(rnd):
            quad = rnd // (BATCH_TILES * QUAD // PAIR)
            t = rnd // (QUAD // PAIR) % BATCH_TILES
            pair = rnd % (QUAD // PAIR)
            first = (t * PLACES + quad * QUAD + pair * PAIR) * P
            nc.vector.quantize_mx(
                out=x_codes[:, first : first + PAIR * P].bitcast(FP8X4),
                scales=x_scales[:, first : first + PAIR * P],
                in_=grouped_tiles[rnd][:],
            )

        def regroup_weights(place):
            own_columns = w_grouped[:, place, :, :]
            by_column = w_raw[:, place, :, :].rearrange("q j c -> q c j")
            if place <= QUAD:
                nc.vector.tensor_copy(out=own_columns, in_=by_column)
            else:
                nc.scalar.copy(out=own_columns, in_=by_column)

        def quantise_weights(place):
            nc.vector.quantize_mx(
                out=w_codes[:, place, 0:COUT].bitcast(FP8X4),
                scales=w_scales[:, place, 0:COUT],
                in_=w_grouped[:, place, :, :].rearrange("q c j -> q (c j)"),
            )

        for rnd in range(LEAD):
            flip(rnd)
            empty(rnd)
            if rnd > 0:
                quantise(rnd - 1)
        spread_bias()
        flip(LEAD)
        empty(LEAD)
        quantise(LEAD - 1)
        acc = {}
        result = {}
        for first, end in GROUPS:
            acc[first] = acc_pool.tile([P, BANK], F32, name="acc%d" % first)
            result[first] = keep.tile([P, BATCH_TILES, (end - first) * COUT], F32, name="result%d" % first)

        def passes(place):
            first, end = [g for g in GROUPS if g[0] <= place < g[1]][0]
            span = (end - first - 1) * COUT + MOVING
            for t in range(BATCH_TILES):
                x_cols = slice((t * PLACES + place) * P, (t * PLACES + place + 1) * P)
                start_col = t * span + (place - first) * COUT
                nc.tensor.matmul_mx(
                    out=acc[first][:, start_col : start_col + MOVING],
                    lhsT=x_codes[:, x_cols].bitcast(FP8X4),
                    lhsT_scale=x_scales[:, x_cols],
                    rhs=w_codes[:, place, :].bitcast(FP8X4),
                    rhs_scale=w_scales[:, place, :],
                    start=True,
                    stop=True,
                )

        def finish(first, end):
            span = (end - first - 1) * COUT + MOVING
            width = (end - first) * COUT
            out_cols = slice(first * COUT, end * COUT)
            nc.vector.tensor_tensor(
                out=result[first][:],
                in0=acc[first][:, 0 : BATCH_TILES * span].rearrange("b (t w) -> b t w", t=BATCH_TILES)[:, :, 0:width],
                in1=bias_all[:, out_cols].unsqueeze(1).to_broadcast([P, BATCH_TILES, width]),
                op=mybir.AluOpType.add,
            )
            nc.sync.dma_start(out=out_rows[:, :, out_cols], in_=result[first][:])


        flip(5)
        empty(5)
        quantise(4)
        flip(6)
        empty(6)
        flip(7)
        empty(7)
        regroup_weights(0)
        regroup_weights(1)
        quantise_weights(0)
        passes(0)
        quantise_weights(1)
        passes(1)
        regroup_weights(2)
        quantise(5)
        quantise_weights(2)
        passes(2)
        regroup_weights(3)
        regroup_weights(4)
        quantise_weights(3)
        passes(3)
        quantise_weights(4)
        quantise(6)
        passes(4)
        regroup_weights(5)
        quantise_weights(5)
        passes(5)
        quantise(7)
        regroup_weights(6)
        quantise_weights(6)
        passes(6)
        regroup_weights(7)
        quantise_weights(7)
        passes(7)
        finish(0, 4)
        finish(4, 7)
        finish(7, 8)
